import numpy as np
import ml_dtypes


def mxq(x, axis, fmt="e4m3"):
    dtype, down = {"e4m3": (ml_dtypes.float8_e4m3fn, 7), "e5m2": (ml_dtypes.float8_e5m2, 14)}[fmt]
    v = np.moveaxis(np.asarray(x, np.float32).astype(ml_dtypes.bfloat16).astype(np.float64), axis, -1)
    blocks = v.reshape(v.shape[:-1] + (-1, 32))
    amax = np.abs(blocks).max(-1, keepdims=True)
    byte = np.maximum(np.where(amax > 0, np.frexp(amax)[1] - 1 + 127, 0) - down, 1)
    scale = np.exp2(byte - 127.0)
    codes = (blocks / scale).astype(np.float32).astype(dtype).astype(np.float64)
    return np.moveaxis((codes * scale).reshape(v.shape), -1, axis)


WIDE = False


def mx_kscale(k):
    if not WIDE:
        return np.ones(k)
    levels = np.array([10, -10, 5, -5, 0])
    a = np.random.permutation(np.resize(levels, k // 512 * 4)).reshape(k // 512, 4)
    idx = np.arange(k)
    return np.exp2(a[idx // 512, idx % 128 // 32])


BF16 = ml_dtypes.bfloat16


def bf(x):
    return np.asarray(x, np.float32).astype(BF16)


def f64(x):
    return np.asarray(x).astype(np.float64)


E2M1 = np.array([0.0, 0.5, 1.0, 1.5, 2.0, 3.0, 4.0, 6.0, -0.0, -0.5, -1.0, -1.5, -2.0, -3.0, -4.0, -6.0])


def pack_weight(w, fmt):
    k, n = w.shape
    w = f64(bf(w)).reshape(k // 32, 32, n)
    amax = np.abs(w).max(1)
    if fmt == "e4m3":
        byte = np.frexp(amax)[1] - 1 + 127 - 7
    else:
        mant, ex = np.frexp(amax / 6.0)
        byte = np.where(mant > 0.5, ex, ex - 1) + 127
    byte = np.clip(np.where(amax > 0, byte, 1), 1, 254)
    scaled = (w * np.exp2(127.0 - byte)[:, None, :]).reshape(k, n).astype(np.float32)
    by_word = np.ascontiguousarray(scaled.reshape(k // 512, 128, 4, n).transpose(0, 1, 3, 2))
    if fmt == "e4m3":
        words = by_word.astype(ml_dtypes.float8_e4m3fn).view(np.uint8)
    else:
        c = by_word.astype(ml_dtypes.float4_e2m1fn).view(np.uint8) & 0xF
        words = c[..., 0::2] | (c[..., 1::2] << 4)
    return np.ascontiguousarray(words), np.ascontiguousarray(byte.astype(np.uint8).reshape(k // 512, 16, n))


def unpack_weight(words, scales, fmt):
    g, p, n, _ = words.shape
    if fmt == "e4m3":
        vals = np.ascontiguousarray(words).view(ml_dtypes.float8_e4m3fn).astype(np.float64)
    else:
        nib = np.empty((g, p, n, 4), np.uint8)
        nib[..., 0::2] = words & 0xF
        nib[..., 1::2] = words >> 4
        vals = E2M1[nib]
    vals = vals * np.repeat(np.exp2(scales.astype(np.float64) - 127.0), 8, axis=1)[..., None]
    return vals.transpose(0, 1, 3, 2).reshape(g * 512, n)


N, M, D = 128, 128, 4096

MIN_NORM = 1e-5
PROJ_EPS = 4e-3


def expmap0(u, c):
    sqrt_c = np.sqrt(c)
    u_norm = np.maximum(np.linalg.norm(u, axis=-1, keepdims=True), MIN_NORM)
    return np.tanh(sqrt_c * u_norm) * u / (sqrt_c * u_norm)


def project(x, c):
    norm = np.maximum(np.linalg.norm(x, axis=-1, keepdims=True), MIN_NORM)
    maxnorm = (1.0 - PROJ_EPS) / np.sqrt(c)
    return np.where(norm > maxnorm, x / norm * maxnorm, x)


def softmax_rows(v):
    e = np.exp(v - v.max(axis=1, keepdims=True))
    return e / e.sum(axis=1, keepdims=True)


def setup_inputs():
    s, t = mx_kscale(D), mx_kscale(D)
    s = s / np.sqrt(np.mean(s * s))
    t = t * np.sqrt(np.mean(1.0 / (t * t)))
    rq = 0.5 + 3.5 * np.random.random_sample((N, 1))
    rc = 0.5 + 3.5 * np.random.random_sample((M, 1))
    query = bf(np.random.standard_normal((N, D)) * rq / np.sqrt(D) * s)
    context = bf(np.random.standard_normal((M, D)) * rc / np.sqrt(D) / t)
    w = np.random.standard_normal((D, D)) * 3.0 * D * t[:, None] / s[None, :]
    W_words, W_scales = pack_weight(w.T, "e4m3")
    c = bf(1.0 + 0.1 * np.random.standard_normal(1))
    return {"query": query,
            "context": context,
            "W_words": W_words,
            "W_scales": W_scales,
            "c": c}


def reference(query, context, W_words, W_scales, c):
    query, context, c = f64(query), f64(context), f64(c)
    n, d = query.shape
    q = project(expmap0(query, c), c)
    ctx = project(expmap0(context, c), c)
    q = mxq(q, 1, "e4m3") @ unpack_weight(W_words, W_scales, "e4m3")
    scores = mxq(q, 1, "e4m3") @ mxq(ctx, 1, "e4m3").T
    attn = softmax_rows(scores / d)
    attn = project(expmap0(attn, c), c)
    return attn

@@ -1,0 +1,358 @@
+from contextlib import ExitStack
+
+import concourse.mybir as mybir
+from concourse.masks import make_identity
+
+F32 = mybir.dt.float32
+BF16 = mybir.dt.bfloat16
+I32 = mybir.dt.int32
+U32 = mybir.dt.uint32
+U8 = mybir.dt.uint8
+FP8X4 = mybir.dt.float8_e4m3fn_x4
+ALU = mybir.AluOpType
+ACT = mybir.ActivationFunctionType
+
+P = 128
+D = 4096
+GROUPS = D // 512
+MIN_NORM = 1e-5
+BALL = 1.0 - 4e-3
+
+FLOPS = 2 * P * D * D + 2 * P * P * D
+
+BANK_OF_RANGE = [1, 2, 3, 4, 0, 5, 6, 7]
+
+PIECES = (
+    [(g, 0, D) for g in range(6)]
+    + [(6, 0, 2048), (6, 2048, D)]
+    + [(7, 0, 1024), (7, 1024, 2048), (7, 2048, 2560), (7, 2560, 3072), (7, 3072, 3584), (7, 3584, D)]
+)
+
+
+def tile_hyphawkes_w_kernel(tc, query, context, W_words, W_scales, c, out):
+    nc = tc.nc
+    with ExitStack() as stack:
+        keep = stack.enter_context(tc.tile_pool(name="keep", bufs=1))
+        psum = stack.enter_context(tc.psum_pool(name="psum", bufs=1))
+        stack.enter_context(tc.manual_schedule())
+
+        def small(name):
+            return keep.tile([P, 1], F32, name=name)
+
+        c_bf = keep.tile([P, 1], BF16, name="c_bf")
+        nc.scalar.dma_start(out=c_bf[:], in_=c.partition_broadcast(P))
+        warm_in = small("warm_in")
+        warm_out = small("warm_out")
+        nc.vector.memset(warm_in[:], 0.0)
+        nc.scalar.activation(out=warm_out[:], in_=warm_in[:], func=ACT.Exp)
+
+        w_planes = keep.tile([P, 2, D], U8, name="w_planes", align_bytes=64)
+        nc.vector.memset(w_planes[:].rearrange("p a n -> p (a n)").bitcast(I32), 0)
+
+        x_sb = {}
+        for name, src in (("q", query), ("c", context)):
+            for h in range(2):
+                x_sb[name, h] = keep.tile([P, 2048], BF16, name="x_%s%d" % (name, h), align_bytes=64)
+                nc.sync.dma_start(out=x_sb[name, h][:], in_=src[:, 2048 * h : 2048 * (h + 1)])
+
+        for a in range(2):
+            for quad in range(4):
+                nc.sync.dma_start(
+                    out=w_planes[32 * quad : 32 * quad + 16, a, :].bitcast(I32),
+                    in_=W_scales[4 * a : 4 * a + 4, 4 * quad : 4 * quad + 4, :].bitcast(I32),
+                )
+
+        w_sb = []
+        for i, (g, n0, n1) in enumerate(PIECES):
+            w_piece = keep.tile([P, n1 - n0], I32, name="w_%d" % i, align_bytes=64)
+            nc.sync.dma_start(
+                out=w_piece[:],
+                in_=W_words[g].rearrange("p n t -> p (n t)").bitcast(I32)[:, n0:n1],
+            )
+            w_sb.append(w_piece)
+
+        ident_f = keep.tile([P, P], F32, name="ident_f")
+        make_identity(nc, ident_f[:])
+        ident_b = keep.tile([P, P], BF16, name="ident_b")
+        make_identity(nc, ident_b[:])
+        half = small("half")
+        nc.gpsimd.memset(half[:], 0.5)
+
+        c_f = small("c_f")
+        root_c = small("root_c")
+        inv_root_c = small("inv_root_c")
+        radius = small("radius")
+        cap = small("cap")
+        gain = small("gain")
+        nc.vector.tensor_copy(out=c_f[:], in_=c_bf[:])
+        nc.gpsimd.tensor_tensor(out=root_c[:], in0=c_f[:], in1=half[:], op=ALU.pow)
+        nc.vector.reciprocal(out=inv_root_c[:], in_=root_c[:])
+        nc.vector.tensor_scalar(out=radius[:], in0=inv_root_c[:], scalar1=BALL, scalar2=None, op0=ALU.mult)
+        nc.vector.tensor_scalar(
+            out=cap[:], in0=radius[:], scalar1=1.0 / MIN_NORM, scalar2=1.0, op0=ALU.mult, op1=ALU.min
+        )
+        nc.vector.tensor_scalar(out=gain[:], in0=cap[:], scalar1=inv_root_c[:, 0:1], scalar2=None, op0=ALU.mult)
+
+        junk = keep.tile([P, 2048], BF16, name="junk")
+        sumsq = keep.tile([P, 4], F32, name="sumsq")
+
+        def square(name, h, col):
+            nc.scalar.activation(
+                out=junk[:], in_=x_sb[name, h][:], func=ACT.Square, accum_out=sumsq[:, col : col + 1]
+            )
+
+        square("q", 0, 0)
+        square("q", 1, 1)
+        square("c", 0, 2)
+
+        q_ps = []
+        for pair in range(4):
+            bank = psum.tile([P, 2, 2, P], F32, name="q_ps%d" % pair, tag="bank%d" % pair)
+            words = x_sb["q", pair // 2][:].bitcast(F32)
+            for gi in range(2):
+                base = 256 * (2 * (pair % 2) + gi)
+                for u in range(2):
+                    nc.tensor.transpose(bank[:, gi, u, :], words[:, base + u : base + 256 : 2], ident_f[:])
+            q_ps.append(bank)
+
+        def transpose_context(pair, tag):
+            bank = psum.tile([P, 2, 4, P], BF16, name="c_ps%d" % pair, tag=tag)
+            for gi in range(2):
+                base = 512 * (2 * (pair % 2) + gi)
+                for t in range(4):
+                    nc.tensor.transpose(
+                        bank[:, gi, t, :],
+                        x_sb["c", pair // 2][:, base + 128 * t : base + 128 * (t + 1)],
+                        ident_b[:],
+                    )
+            return bank
+
+        c_ps = [transpose_context(pair, "bank%d" % (5 + pair)) for pair in range(3)]
+
+        tiles = {}
+        for name in ("q", "c"):
+            for part in ("m", "r", "th", "rr", "t2", "s"):
+                tiles[name, part] = small("%s_%s" % (part, name))
+            tiles[name, "spread"] = keep.tile([P, P], F32, name="spread_%s" % name)
+
+        def factor_a(name, col):
+            nc.vector.tensor_scalar(
+                out=tiles[name, "m"][:],
+                in0=sumsq[:, col : col + 1],
+                scalar1=sumsq[:, col + 1 : col + 2],
+                scalar2=MIN_NORM * MIN_NORM,
+                op0=ALU.add,
+                op1=ALU.max,
+            )
+            nc.gpsimd.tensor_tensor(out=tiles[name, "r"][:], in0=tiles[name, "m"][:], in1=half[:], op=ALU.pow)
+            nc.scalar.activation(
+                out=tiles[name, "th"][:], in_=tiles[name, "r"][:], func=ACT.Tanh, scale=root_c[:, 0:1]
+            )
+
+        def factor_b(name):
+            nc.vector.reciprocal(out=tiles[name, "rr"][:], in_=tiles[name, "r"][:])
+
+        def factor_c(name):
+            nc.vector.tensor_scalar(
+                out=tiles[name, "t2"][:],
+                in0=tiles[name, "th"][:],
+                scalar1=gain[:, 0:1],
+                scalar2=radius[:, 0:1],
+                op0=ALU.mult,
+                op1=ALU.min,
+            )
+            nc.vector.tensor_scalar(
+                out=tiles[name, "s"][:],
+                in0=tiles[name, "t2"][:],
+                scalar1=tiles[name, "rr"][:, 0:1],
+                scalar2=None,
+                op0=ALU.mult,
+            )
+            spread_ps = psum.tile([P, P], F32, name="spread_ps_%s" % name, tag="bank4")
+            nc.tensor.matmul(
+                out=spread_ps[:],
+                lhsT=tiles[name, "s"][:, 0:1].to_broadcast([P, P]),
+                rhs=ident_f[:],
+                start=True,
+                stop=True,
+            )
+            return spread_ps
+
+        def factor_d(name, spread_ps):
+            nc.vector.tensor_copy(out=tiles[name, "spread"][:], in_=spread_ps[:])
+
+        q_grouped = keep.tile([P, GROUPS, 512], BF16, name="q_grouped", align_bytes=64)
+        q_codes = keep.tile([P, GROUPS, P], U32, name="q_codes", align_bytes=64)
+        q_plane = keep.tile([P, GROUPS, P], U8, name="q_plane", align_bytes=64)
+        c_grouped = keep.tile([P, GROUPS, 512], BF16, name="c_grouped", align_bytes=64)
+        c_codes = keep.tile([P, GROUPS, P], U32, name="c_codes", align_bytes=64)
+        c_plane = keep.tile([P, GROUPS, P], U8, name="c_plane", align_bytes=64)
+
+        def scale_query(g):
+            nc.vector.tensor_tensor(
+                out=q_grouped[:, g, :].rearrange("p (r u e) -> p r u e", u=2, e=2),
+                in0=q_ps[g // 2][:, g % 2].bitcast(BF16).rearrange("p u (r e) -> p r u e", e=2),
+                in1=tiles["q", "spread"][:].unsqueeze(2).unsqueeze(3).to_broadcast([P, P, 2, 2]),
+                op=ALU.mult,
+            )
+
+        def scale_context(pair, bank):
+            nc.vector.tensor_tensor(
+                out=c_grouped[:, 2 * pair : 2 * pair + 2, :].rearrange("p g (r t) -> p g r t", t=4),
+                in0=bank[:].rearrange("p g t r -> p g r t"),
+                in1=tiles["c", "spread"][:].unsqueeze(1).unsqueeze(3).to_broadcast([P, 2, P, 4]),
+                op=ALU.mult,
+            )
+
+        def quantise_half(grouped, codes, plane, h):
+            sel = slice(4 * h, 4 * h + 4)
+            nc.vector.quantize_mx(
+                out=codes[:, sel, :].rearrange("p g r -> p (g r)").bitcast(FP8X4),
+                scales=plane[:, sel, :].rearrange("p g r -> p (g r)"),
+                in_=grouped[:, sel, :].rearrange("p g x -> p (g x)"),
+            )
+
+        factor_a("q", 0)
+        square("c", 1, 3)
+        factor_b("q")
+        spread_q = factor_c("q")
+        factor_d("q", spread_q)
+        scale_query(0)
+        scale_query(1)
+        c_ps.append(transpose_context(3, "bank0"))
+        scale_query(2)
+        scale_query(3)
+        factor_a("c", 2)
+        scale_query(4)
+        quantise_half(q_grouped, q_codes, q_plane, 0)
+        factor_b("c")
+        scale_query(5)
+        spread_c = factor_c("c")
+        scale_query(6)
+        scale_query(7)
+        factor_d("c", spread_c)
+        quantise_half(q_grouped, q_codes, q_plane, 1)
+        scale_context(3, c_ps[3])
+        scale_context(0, c_ps[0])
+        scale_context(1, c_ps[1])
+        scale_context(2, c_ps[2])
+        quantise_half(c_grouped, c_codes, c_plane, 0)
+        quantise_half(c_grouped, c_codes, c_plane, 1)
+
+        h_ps = [
+            psum.tile([P, 4, P], F32, name="h_ps%d" % j, tag="bank%d" % BANK_OF_RANGE[j]) for j in range(GROUPS)
+        ]
+
+        def first_matmul(i):
+            g, n0, n1 = PIECES[i]
+            for j in range(n0 // 512, n1 // 512):
+                for t in range(4):
+                    col = 512 * j + 128 * t
+                    nc.tensor.matmul_mx(
+                        out=h_ps[j][:, t, :],
+                        lhsT=w_sb[i][:, col - n0 : col - n0 + P].bitcast(FP8X4),
+                        lhsT_scale=w_planes[4 * (g % 4) : P, g // 4, col : col + P],
+                        rhs=q_codes[:, g, :].bitcast(FP8X4),
+                        rhs_scale=q_plane[:, g, :],
+                        start=(g == 0 and t == 0),
+                        stop=(g == GROUPS - 1 and t == 3),
+                    )
+
+        h_grouped = [keep.tile([P, P, 4], BF16, name="h_grouped%d" % j, align_bytes=64) for j in range(GROUPS)]
+        h_codes = [keep.tile([P, P], U32, name="h_codes%d" % j, align_bytes=64) for j in range(GROUPS)]
+        h_plane = [keep.tile([P, P], U8, name="h_plane%d" % j, align_bytes=64) for j in range(GROUPS)]
+
+        def round_h(j):
+            src = h_ps[j][:].rearrange("p t r -> p r t")
+            if j % 2 == 0:
+                nc.vector.tensor_copy(out=h_grouped[j][:], in_=src)
+            else:
+                nc.scalar.copy(out=h_grouped[j][:], in_=src)
+
+        def quantise_h(j):
+            nc.vector.quantize_mx(
+                out=h_codes[j][:].bitcast(FP8X4),
+                scales=h_plane[j][:],
+                in_=h_grouped[j][:].rearrange("p r t -> p (r t)"),
+            )
+
+        scores = []
+
+        def second_matmul(j):
+            if j == 0:
+                scores.append(psum.tile([P, P], F32, name="scores", tag="bank%d" % BANK_OF_RANGE[0]))
+            nc.tensor.matmul_mx(
+                out=scores[0][:],
+                lhsT=h_codes[j][:].bitcast(FP8X4),
+                lhsT_scale=h_plane[j][:],
+                rhs=c_codes[:, j, :].bitcast(FP8X4),
+                rhs_scale=c_plane[:, j, :],
+                start=(j == 0),
+                stop=(j == GROUPS - 1),
+            )
+
+        for i in range(8):
+            first_matmul(i)
+        first_matmul(8)
+        round_h(0)
+        round_h(1)
+        first_matmul(9)
+        quantise_h(0)
+        quantise_h(1)
+        round_h(2)
+        round_h(3)
+        second_matmul(0)
+        second_matmul(1)
+        first_matmul(10)
+        first_matmul(11)
+        quantise_h(2)
+        quantise_h(3)
+        round_h(4)
+        round_h(5)
+        second_matmul(2)
+        second_matmul(3)
+        first_matmul(12)
+        first_matmul(13)
+        quantise_h(4)
+        quantise_h(5)
+        round_h(6)
+        round_h(7)
+        second_matmul(4)
+        second_matmul(5)
+        quantise_h(6)
+        quantise_h(7)
+        second_matmul(6)
+        second_matmul(7)
+
+        neg = keep.tile([P, P], F32, name="neg")
+        e = keep.tile([P, P], F32, name="e")
+        e2 = keep.tile([P, P], F32, name="e2")
+        res = keep.tile([P, P], F32, name="res")
+        shift = small("shift")
+        total = small("total")
+        total2 = small("total2")
+        root2 = small("root2")
+        inv_total = small("inv_total")
+        arg_scale = small("arg_scale")
+        th = small("th")
+        inv_root2 = small("inv_root2")
+        lim = small("lim")
+        nc.vector.tensor_scalar(
+            out=neg[:], in0=scores[0][:], scalar1=-1.0 / D, scalar2=None, op0=ALU.mult, op1=ALU.min, accum_out=shift[:]
+        )
+        nc.scalar.activation(out=e[:], in_=neg[:], func=ACT.Exp, scale=-1.0, bias=shift[:, 0:1], accum_out=total[:])
+        nc.scalar.activation(out=e2[:], in_=e[:], func=ACT.Square, accum_out=total2[:])
+        nc.vector.reciprocal(out=inv_total[:], in_=total[:])
+        nc.vector.tensor_scalar(
+            out=arg_scale[:], in0=inv_total[:], scalar1=root_c[:, 0:1], scalar2=None, op0=ALU.mult
+        )
+        nc.gpsimd.tensor_tensor(out=root2[:], in0=total2[:], in1=half[:], op=ALU.pow)
+        nc.scalar.activation(out=th[:], in_=root2[:], func=ACT.Tanh, scale=arg_scale[:, 0:1])
+        nc.vector.reciprocal(out=inv_root2[:], in_=root2[:])
+        nc.vector.tensor_scalar(
+            out=lim[:], in0=th[:], scalar1=gain[:, 0:1], scalar2=radius[:, 0:1], op0=ALU.mult, op1=ALU.min
+        )
+        nc.vector.tensor_scalar(
+            out=res[:], in0=e[:], scalar1=lim[:, 0:1], scalar2=inv_root2[:, 0:1], op0=ALU.mult, op1=ALU.mult
+        )
+        nc.sync.dma_start(out=out[:, :], in_=res[:])

@@ -55,11 +55,11 @@ def tile_hyphawkes_w_kernel(tc, query, context, W_words, W_scales, c, out):
                 x_sb[name, h] = keep.tile([P, 2048], BF16, name="x_%s%d" % (name, h), align_bytes=64)
                 nc.sync.dma_start(out=x_sb[name, h][:], in_=src[:, 2048 * h : 2048 * (h + 1)])
 
-        for a in range(2):
-            for quad in range(4):
-                nc.sync.dma_start(
-                    out=w_planes[32 * quad : 32 * quad + 16, a, :].bitcast(I32),
-                    in_=W_scales[4 * a : 4 * a + 4, 4 * quad : 4 * quad + 4, :].bitcast(I32),
+        def load_planes(a):
+            for quad in (0, 2, 1, 3):
+                nc.gpsimd.dma_start(
+                    out=w_planes[32 * quad : 32 * quad + 16, a, :].bitcast(F32),
+                    in_=W_scales[4 * a : 4 * a + 4, 4 * quad : 4 * quad + 4, :].bitcast(F32),
                 )
 
         w_sb = []
@@ -77,6 +77,9 @@ def tile_hyphawkes_w_kernel(tc, query, context, W_words, W_scales, c, out):
         make_identity(nc, ident_b[:])
         half = small("half")
         nc.gpsimd.memset(half[:], 0.5)
+        neg_half = small("neg_half")
+        nc.gpsimd.memset(neg_half[:], -0.5)
+        load_planes(0)
 
         c_f = small("c_f")
         root_c = small("root_c")
@@ -213,6 +216,7 @@ def tile_hyphawkes_w_kernel(tc, query, context, W_words, W_scales, c, out):
             )
 
         factor_a("q", 0)
+        load_planes(1)
         square("c", 1, 3)
         factor_b("q")
         spread_q = factor_c("q")
@@ -331,12 +335,13 @@ def tile_hyphawkes_w_kernel(tc, query, context, W_words, W_scales, c, out):
         shift = small("shift")
         total = small("total")
         total2 = small("total2")
-        root2 = small("root2")
+        arg2 = small("arg2")
+        e_gain = keep.tile([P, P], F32, name="e_gain")
+        e_cap = keep.tile([P, P], F32, name="e_cap")
         inv_total = small("inv_total")
         arg_scale = small("arg_scale")
         th = small("th")
         inv_root2 = small("inv_root2")
-        lim = small("lim")
         nc.vector.tensor_scalar(
             out=neg[:], in0=scores[0][:], scalar1=-1.0 / D, scalar2=None, op0=ALU.mult, op1=ALU.min, accum_out=shift[:]
         )
@@ -346,13 +351,18 @@ def tile_hyphawkes_w_kernel(tc, query, context, W_words, W_scales, c, out):
         nc.vector.tensor_scalar(
             out=arg_scale[:], in0=inv_total[:], scalar1=root_c[:, 0:1], scalar2=None, op0=ALU.mult
         )
-        nc.gpsimd.tensor_tensor(out=root2[:], in0=total2[:], in1=half[:], op=ALU.pow)
-        nc.scalar.activation(out=th[:], in_=root2[:], func=ACT.Tanh, scale=arg_scale[:, 0:1])
-        nc.vector.reciprocal(out=inv_root2[:], in_=root2[:])
+        nc.gpsimd.tensor_tensor(out=inv_root2[:], in0=total2[:], in1=neg_half[:], op=ALU.pow)
         nc.vector.tensor_scalar(
-            out=lim[:], in0=th[:], scalar1=gain[:, 0:1], scalar2=radius[:, 0:1], op0=ALU.mult, op1=ALU.min
+            out=arg2[:], in0=total2[:], scalar1=arg_scale[:, 0:1], scalar2=None, op0=ALU.mult
+        )
+        nc.scalar.activation(out=th[:], in_=inv_root2[:], func=ACT.Tanh, scale=arg2[:, 0:1])
+        nc.vector.tensor_scalar(
+            out=e_gain[:], in0=e[:], scalar1=gain[:, 0:1], scalar2=inv_root2[:, 0:1], op0=ALU.mult, op1=ALU.mult
         )
         nc.vector.tensor_scalar(
-            out=res[:], in0=e[:], scalar1=lim[:, 0:1], scalar2=inv_root2[:, 0:1], op0=ALU.mult, op1=ALU.mult
+            out=e_cap[:], in0=e[:], scalar1=radius[:, 0:1], scalar2=inv_root2[:, 0:1], op0=ALU.mult, op1=ALU.mult
+        )
+        nc.vector.scalar_tensor_tensor(
+            out=res[:], in0=e_gain[:], scalar=th[:, 0:1], in1=e_cap[:], op0=ALU.mult, op1=ALU.min
         )
         nc.sync.dma_start(out=out[:, :], in_=res[:])

@@ -20,7 +20,7 @@ BALL = 1.0 - 4e-3
 
 FLOPS = 2 * P * D * D + 2 * P * P * D
 
-BANK_OF_RANGE = [1, 2, 3, 4, 0, 5, 6, 7]
+BANK_OF_RANGE = [5, 6, 4, 0, 1, 2, 3, 7]
 
 PIECES = (
     [(g, 0, D) for g in range(6)]
@@ -57,10 +57,13 @@ def tile_hyphawkes_w_kernel(tc, query, context, W_words, W_scales, c, out):
 
         def load_planes(a):
             for quad in (0, 2, 1, 3):
-                nc.gpsimd.dma_start(
-                    out=w_planes[32 * quad : 32 * quad + 16, a, :].bitcast(F32),
-                    in_=W_scales[4 * a : 4 * a + 4, 4 * quad : 4 * quad + 4, :].bitcast(F32),
+                nc.sync.dma_start(
+                    out=w_planes[32 * quad : 32 * quad + 16, a, :].bitcast(I32),
+                    in_=W_scales[4 * a : 4 * a + 4, 4 * quad : 4 * quad + 4, :].bitcast(I32),
                 )
+
+        load_planes(0)
+        load_planes(1)
 
         w_sb = []
         for i, (g, n0, n1) in enumerate(PIECES):
@@ -79,7 +82,6 @@ def tile_hyphawkes_w_kernel(tc, query, context, W_words, W_scales, c, out):
         nc.gpsimd.memset(half[:], 0.5)
         neg_half = small("neg_half")
         nc.gpsimd.memset(neg_half[:], -0.5)
-        load_planes(0)
 
         c_f = small("c_f")
         root_c = small("root_c")
@@ -106,7 +108,6 @@ def tile_hyphawkes_w_kernel(tc, query, context, W_words, W_scales, c, out):
 
         square("q", 0, 0)
         square("q", 1, 1)
-        square("c", 0, 2)
 
         q_ps = []
         for pair in range(4):
@@ -129,8 +130,6 @@ def tile_hyphawkes_w_kernel(tc, query, context, W_words, W_scales, c, out):
                         ident_b[:],
                     )
             return bank
-
-        c_ps = [transpose_context(pair, "bank%d" % (5 + pair)) for pair in range(3)]
 
         tiles = {}
         for name in ("q", "c"):
@@ -155,7 +154,7 @@ def tile_hyphawkes_w_kernel(tc, query, context, W_words, W_scales, c, out):
         def factor_b(name):
             nc.vector.reciprocal(out=tiles[name, "rr"][:], in_=tiles[name, "r"][:])
 
-        def factor_c(name):
+        def factor_c(name, tag):
             nc.vector.tensor_scalar(
                 out=tiles[name, "t2"][:],
                 in0=tiles[name, "th"][:],
@@ -171,7 +170,7 @@ def tile_hyphawkes_w_kernel(tc, query, context, W_words, W_scales, c, out):
                 scalar2=None,
                 op0=ALU.mult,
             )
-            spread_ps = psum.tile([P, P], F32, name="spread_ps_%s" % name, tag="bank4")
+            spread_ps = psum.tile([P, P], F32, name="spread_ps_%s" % name, tag=tag)
             nc.tensor.matmul(
                 out=spread_ps[:],
                 lhsT=tiles[name, "s"][:, 0:1].to_broadcast([P, P]),
@@ -216,40 +215,27 @@ def tile_hyphawkes_w_kernel(tc, query, context, W_words, W_scales, c, out):
             )
 
         factor_a("q", 0)
-        load_planes(1)
+        square("c", 0, 2)
         square("c", 1, 3)
         factor_b("q")
-        spread_q = factor_c("q")
+        spread_q = factor_c("q", "bank4")
         factor_d("q", spread_q)
-        scale_query(0)
-        scale_query(1)
-        c_ps.append(transpose_context(3, "bank0"))
-        scale_query(2)
-        scale_query(3)
-        factor_a("c", 2)
-        scale_query(4)
+        for g in range(5):
+            scale_query(g)
         quantise_half(q_grouped, q_codes, q_plane, 0)
-        factor_b("c")
-        scale_query(5)
-        spread_c = factor_c("c")
-        scale_query(6)
-        scale_query(7)
-        factor_d("c", spread_c)
+        for g in range(5, GROUPS):
+            scale_query(g)
+        factor_a("c", 2)
         quantise_half(q_grouped, q_codes, q_plane, 1)
-        scale_context(3, c_ps[3])
-        scale_context(0, c_ps[0])
-        scale_context(1, c_ps[1])
-        scale_context(2, c_ps[2])
-        quantise_half(c_grouped, c_codes, c_plane, 0)
-        quantise_half(c_grouped, c_codes, c_plane, 1)
+        factor_b("c")
 
-        h_ps = [
-            psum.tile([P, 4, P], F32, name="h_ps%d" % j, tag="bank%d" % BANK_OF_RANGE[j]) for j in range(GROUPS)
-        ]
+        h_ps = {}
 
-        def first_matmul(i):
+        def first_matmul(i, ranges):
             g, n0, n1 = PIECES[i]
-            for j in range(n0 // 512, n1 // 512):
+            for j in ranges:
+                if g == 0:
+                    h_ps[j] = psum.tile([P, 4, P], F32, name="h_ps%d" % j, tag="bank%d" % BANK_OF_RANGE[j])
                 for t in range(4):
                     col = 512 * j + 128 * t
                     nc.tensor.matmul_mx(
@@ -295,28 +281,41 @@ def tile_hyphawkes_w_kernel(tc, query, context, W_words, W_scales, c, out):
                 stop=(j == GROUPS - 1),
             )
 
-        for i in range(8):
-            first_matmul(i)
-        first_matmul(8)
+        first_matmul(0, range(7))
+        spread_c = factor_c("c", "bank7")
+        factor_d("c", spread_c)
+        for pair in range(4):
+            if pair > 0:
+                first_matmul(pair, range(7))
+            scale_context(pair, transpose_context(pair, "bank7"))
+        quantise_half(c_grouped, c_codes, c_plane, 0)
+        quantise_half(c_grouped, c_codes, c_plane, 1)
+        for i in range(4):
+            first_matmul(i, [7])
+        first_matmul(4, range(8))
+        first_matmul(5, range(8))
+        first_matmul(6, range(4))
+        first_matmul(7, range(4, 8))
+        first_matmul(8, [0, 1])
         round_h(0)
         round_h(1)
-        first_matmul(9)
+        first_matmul(9, [2, 3])
         quantise_h(0)
         quantise_h(1)
         round_h(2)
         round_h(3)
         second_matmul(0)
         second_matmul(1)
-        first_matmul(10)
-        first_matmul(11)
+        first_matmul(10, [4])
+        first_matmul(11, [5])
         quantise_h(2)
         quantise_h(3)
         round_h(4)
         round_h(5)
         second_matmul(2)
         second_matmul(3)
-        first_matmul(12)
-        first_matmul(13)
+        first_matmul(12, [6])
+        first_matmul(13, [7])
         quantise_h(4)
         quantise_h(5)
         round_h(6)

@@ -24,8 +24,7 @@ BANK_OF_RANGE = [5, 6, 4, 0, 1, 2, 3, 7]
 
 PIECES = (
     [(g, 0, D) for g in range(6)]
-    + [(6, 0, 2048), (6, 2048, D)]
-    + [(7, 0, 1024), (7, 1024, 2048), (7, 2048, 2560), (7, 2560, 3072), (7, 3072, 3584), (7, 3584, D)]
+    + [(6, 0, 2048), (7, 0, 2048), (6, 2048, 3072), (7, 2048, 3072), (6, 3072, D), (7, 3072, 3584), (7, 3584, 3968), (7, 3968, D)]
 )
 
 
@@ -238,6 +237,8 @@ def tile_hyphawkes_w_kernel(tc, query, context, W_words, W_scales, c, out):
                     h_ps[j] = psum.tile([P, 4, P], F32, name="h_ps%d" % j, tag="bank%d" % BANK_OF_RANGE[j])
                 for t in range(4):
                     col = 512 * j + 128 * t
+                    if col < n0 or col >= n1:
+                        continue
                     nc.tensor.matmul_mx(
                         out=h_ps[j][:, t, :],
                         lhsT=w_sb[i][:, col - n0 : col - n0 + P].bitcast(FP8X4),
@@ -295,33 +296,33 @@ def tile_hyphawkes_w_kernel(tc, query, context, W_words, W_scales, c, out):
         first_matmul(4, range(8))
         first_matmul(5, range(8))
         first_matmul(6, range(4))
-        first_matmul(7, range(4, 8))
-        first_matmul(8, [0, 1])
+        first_matmul(7, range(4))
         round_h(0)
         round_h(1)
-        first_matmul(9, [2, 3])
-        quantise_h(0)
-        quantise_h(1)
         round_h(2)
         round_h(3)
+        first_matmul(8, [4, 5])
+        quantise_h(0)
+        quantise_h(1)
         second_matmul(0)
         second_matmul(1)
-        first_matmul(10, [4])
-        first_matmul(11, [5])
+        first_matmul(9, [4, 5])
         quantise_h(2)
         quantise_h(3)
-        round_h(4)
-        round_h(5)
         second_matmul(2)
         second_matmul(3)
-        first_matmul(12, [6])
-        first_matmul(13, [7])
+        round_h(4)
+        round_h(5)
+        first_matmul(10, [6, 7])
+        first_matmul(11, [6])
         quantise_h(4)
         quantise_h(5)
-        round_h(6)
-        round_h(7)
         second_matmul(4)
         second_matmul(5)
+        first_matmul(12, [7])
+        first_matmul(13, [7])
+        round_h(6)
+        round_h(7)
         quantise_h(6)
         quantise_h(7)
         second_matmul(6)
@@ -335,6 +336,7 @@ def tile_hyphawkes_w_kernel(tc, query, context, W_words, W_scales, c, out):
         total = small("total")
         total2 = small("total2")
         arg2 = small("arg2")
+        shift1 = small("shift1")
         e_gain = keep.tile([P, P], F32, name="e_gain")
         e_cap = keep.tile([P, P], F32, name="e_cap")
         inv_total = small("inv_total")
@@ -342,17 +344,18 @@ def tile_hyphawkes_w_kernel(tc, query, context, W_words, W_scales, c, out):
         th = small("th")
         inv_root2 = small("inv_root2")
         nc.vector.tensor_scalar(
-            out=neg[:], in0=scores[0][:], scalar1=-1.0 / D, scalar2=None, op0=ALU.mult, op1=ALU.min, accum_out=shift[:]
+            out=neg[:], in0=scores[0][:], scalar1=-2.0 / D, scalar2=None, op0=ALU.mult, op1=ALU.min, accum_out=shift[:]
         )
-        nc.scalar.activation(out=e[:], in_=neg[:], func=ACT.Exp, scale=-1.0, bias=shift[:, 0:1], accum_out=total[:])
-        nc.scalar.activation(out=e2[:], in_=e[:], func=ACT.Square, accum_out=total2[:])
-        nc.vector.reciprocal(out=inv_total[:], in_=total[:])
-        nc.vector.tensor_scalar(
-            out=arg_scale[:], in0=inv_total[:], scalar1=root_c[:, 0:1], scalar2=None, op0=ALU.mult
-        )
+        nc.scalar.activation(out=e2[:], in_=neg[:], func=ACT.Exp, scale=-1.0, bias=shift[:, 0:1], accum_out=total2[:])
+        nc.vector.tensor_scalar(out=shift1[:], in0=shift[:], scalar1=0.5, scalar2=None, op0=ALU.mult)
+        nc.scalar.activation(out=e[:], in_=neg[:], func=ACT.Exp, scale=-0.5, bias=shift1[:, 0:1], accum_out=total[:])
         nc.gpsimd.tensor_tensor(out=inv_root2[:], in0=total2[:], in1=neg_half[:], op=ALU.pow)
         nc.vector.tensor_scalar(
-            out=arg2[:], in0=total2[:], scalar1=arg_scale[:, 0:1], scalar2=None, op0=ALU.mult
+            out=arg_scale[:], in0=total2[:], scalar1=root_c[:, 0:1], scalar2=None, op0=ALU.mult
+        )
+        nc.vector.reciprocal(out=inv_total[:], in_=total[:])
+        nc.vector.tensor_scalar(
+            out=arg2[:], in0=inv_total[:], scalar1=arg_scale[:, 0:1], scalar2=None, op0=ALU.mult
         )
         nc.scalar.activation(out=th[:], in_=inv_root2[:], func=ACT.Tanh, scale=arg2[:, 0:1])
         nc.vector.tensor_scalar(

@@ -20,10 +20,10 @@ BALL = 1.0 - 4e-3
 
 FLOPS = 2 * P * D * D + 2 * P * P * D
 
-BANK_OF_RANGE = [5, 6, 4, 0, 1, 2, 3, 7]
+BANK_OF_RANGE = [4, 5, 6, 0, 1, 2, 3, 7]
 
 PIECES = (
-    [(g, 0, D) for g in range(6)]
+    [(g, n0, n0 + 2048) for g in range(6) for n0 in (0, 2048)]
     + [(6, 0, 2048), (7, 0, 2048), (6, 2048, 3072), (7, 2048, 3072), (6, 3072, D), (7, 3072, 3584), (7, 3584, 3968), (7, 3968, D)]
 )
 
@@ -46,10 +46,13 @@ def tile_hyphawkes_w_kernel(tc, query, context, W_words, W_scales, c, out):
         nc.scalar.activation(out=warm_out[:], in_=warm_in[:], func=ACT.Exp)
 
         w_planes = keep.tile([P, 2, D], U8, name="w_planes", align_bytes=64)
-        nc.vector.memset(w_planes[:].rearrange("p a n -> p (a n)").bitcast(I32), 0)
+        for a in range(2):
+            nc.vector.memset(w_planes[:, a, :].bitcast(I32), 0)
 
         x_sb = {}
-        for name, src in (("q", query), ("c", context)):
+        w_sb = []
+
+        def load_x(name, src):
             for h in range(2):
                 x_sb[name, h] = keep.tile([P, 2048], BF16, name="x_%s%d" % (name, h), align_bytes=64)
                 nc.sync.dma_start(out=x_sb[name, h][:], in_=src[:, 2048 * h : 2048 * (h + 1)])
@@ -61,17 +64,23 @@ def tile_hyphawkes_w_kernel(tc, query, context, W_words, W_scales, c, out):
                     in_=W_scales[4 * a : 4 * a + 4, 4 * quad : 4 * quad + 4, :].bitcast(I32),
                 )
 
-        load_planes(0)
-        load_planes(1)
-
-        w_sb = []
-        for i, (g, n0, n1) in enumerate(PIECES):
+        def load_words(i):
+            g, n0, n1 = PIECES[i]
             w_piece = keep.tile([P, n1 - n0], I32, name="w_%d" % i, align_bytes=64)
             nc.sync.dma_start(
                 out=w_piece[:],
                 in_=W_words[g].rearrange("p n t -> p (n t)").bitcast(I32)[:, n0:n1],
             )
             w_sb.append(w_piece)
+
+        load_x("q", query)
+        load_planes(0)
+        load_words(0)
+        load_words(1)
+        load_x("c", context)
+        load_planes(1)
+        for i in range(2, len(PIECES)):
+            load_words(i)
 
         ident_f = keep.tile([P, P], F32, name="ident_f")
         make_identity(nc, ident_f[:])
@@ -98,49 +107,32 @@ def tile_hyphawkes_w_kernel(tc, query, context, W_words, W_scales, c, out):
         nc.vector.tensor_scalar(out=gain[:], in0=cap[:], scalar1=inv_root_c[:, 0:1], scalar2=None, op0=ALU.mult)
 
         junk = keep.tile([P, 2048], BF16, name="junk")
-        sumsq = keep.tile([P, 4], F32, name="sumsq")
-
-        def square(name, h, col):
-            nc.scalar.activation(
-                out=junk[:], in_=x_sb[name, h][:], func=ACT.Square, accum_out=sumsq[:, col : col + 1]
-            )
-
-        square("q", 0, 0)
-        square("q", 1, 1)
-
-        q_ps = []
-        for pair in range(4):
-            bank = psum.tile([P, 2, 2, P], F32, name="q_ps%d" % pair, tag="bank%d" % pair)
-            words = x_sb["q", pair // 2][:].bitcast(F32)
-            for gi in range(2):
-                base = 256 * (2 * (pair % 2) + gi)
-                for u in range(2):
-                    nc.tensor.transpose(bank[:, gi, u, :], words[:, base + u : base + 256 : 2], ident_f[:])
-            q_ps.append(bank)
-
-        def transpose_context(pair, tag):
-            bank = psum.tile([P, 2, 4, P], BF16, name="c_ps%d" % pair, tag=tag)
-            for gi in range(2):
-                base = 512 * (2 * (pair % 2) + gi)
-                for t in range(4):
-                    nc.tensor.transpose(
-                        bank[:, gi, t, :],
-                        x_sb["c", pair // 2][:, base + 128 * t : base + 128 * (t + 1)],
-                        ident_b[:],
-                    )
-            return bank
-
+        junk_v = keep.tile([P, 2048], BF16, name="junk_v")
+        sumsq = {}
         tiles = {}
         for name in ("q", "c"):
+            sumsq[name, 0] = small("sumsq_%s0" % name)
+            sumsq[name, 1] = small("sumsq_%s1" % name)
             for part in ("m", "r", "th", "rr", "t2", "s"):
                 tiles[name, part] = small("%s_%s" % (part, name))
-            tiles[name, "spread"] = keep.tile([P, P], F32, name="spread_%s" % name)
 
-        def factor_a(name, col):
+        def square(name):
+            nc.scalar.activation(out=junk[:], in_=x_sb[name, 0][:], func=ACT.Square, accum_out=sumsq[name, 0][:])
+            nc.vector.scalar_tensor_tensor(
+                out=junk_v[:],
+                in0=x_sb[name, 1][:],
+                scalar=1.0,
+                in1=x_sb[name, 1][:],
+                op0=ALU.mult,
+                op1=ALU.mult,
+                accum_out=sumsq[name, 1][:],
+            )
+
+        def factor(name):
             nc.vector.tensor_scalar(
                 out=tiles[name, "m"][:],
-                in0=sumsq[:, col : col + 1],
-                scalar1=sumsq[:, col + 1 : col + 2],
+                in0=sumsq[name, 0][:],
+                scalar1=sumsq[name, 1][:, 0:1],
                 scalar2=MIN_NORM * MIN_NORM,
                 op0=ALU.add,
                 op1=ALU.max,
@@ -149,11 +141,7 @@ def tile_hyphawkes_w_kernel(tc, query, context, W_words, W_scales, c, out):
             nc.scalar.activation(
                 out=tiles[name, "th"][:], in_=tiles[name, "r"][:], func=ACT.Tanh, scale=root_c[:, 0:1]
             )
-
-        def factor_b(name):
             nc.vector.reciprocal(out=tiles[name, "rr"][:], in_=tiles[name, "r"][:])
-
-        def factor_c(name, tag):
             nc.vector.tensor_scalar(
                 out=tiles[name, "t2"][:],
                 in0=tiles[name, "th"][:],
@@ -169,18 +157,14 @@ def tile_hyphawkes_w_kernel(tc, query, context, W_words, W_scales, c, out):
                 scalar2=None,
                 op0=ALU.mult,
             )
-            spread_ps = psum.tile([P, P], F32, name="spread_ps_%s" % name, tag=tag)
-            nc.tensor.matmul(
-                out=spread_ps[:],
-                lhsT=tiles[name, "s"][:, 0:1].to_broadcast([P, P]),
-                rhs=ident_f[:],
-                start=True,
-                stop=True,
-            )
-            return spread_ps
 
-        def factor_d(name, spread_ps):
-            nc.vector.tensor_copy(out=tiles[name, "spread"][:], in_=spread_ps[:])
+        y_sb = {}
+
+        def scale(name, h):
+            y_sb[name, h] = keep.tile([P, 2048], BF16, name="y_%s%d" % (name, h), align_bytes=64)
+            nc.vector.tensor_scalar(
+                out=y_sb[name, h][:], in0=x_sb[name, h][:], scalar1=tiles[name, "s"][:, 0:1], scalar2=None, op0=ALU.mult
+            )
 
         q_grouped = keep.tile([P, GROUPS, 512], BF16, name="q_grouped", align_bytes=64)
         q_codes = keep.tile([P, GROUPS, P], U32, name="q_codes", align_bytes=64)
@@ -189,21 +173,42 @@ def tile_hyphawkes_w_kernel(tc, query, context, W_words, W_scales, c, out):
         c_codes = keep.tile([P, GROUPS, P], U32, name="c_codes", align_bytes=64)
         c_plane = keep.tile([P, GROUPS, P], U8, name="c_plane", align_bytes=64)
 
-        def scale_query(g):
-            nc.vector.tensor_tensor(
-                out=q_grouped[:, g, :].rearrange("p (r u e) -> p r u e", u=2, e=2),
-                in0=q_ps[g // 2][:, g % 2].bitcast(BF16).rearrange("p u (r e) -> p r u e", e=2),
-                in1=tiles["q", "spread"][:].unsqueeze(2).unsqueeze(3).to_broadcast([P, P, 2, 2]),
-                op=ALU.mult,
-            )
+        def transpose_query(pair):
+            bank = psum.tile([P, 2, 2, P], F32, name="q_ps%d" % pair, tag="bank%d" % pair)
+            words = y_sb["q", pair // 2][:].bitcast(F32)
+            for gi in range(2):
+                base = 256 * (2 * (pair % 2) + gi)
+                for u in range(2):
+                    nc.tensor.transpose(bank[:, gi, u, :], words[:, base + u : base + 256 : 2], ident_f[:])
+            return bank
 
-        def scale_context(pair, bank):
-            nc.vector.tensor_tensor(
-                out=c_grouped[:, 2 * pair : 2 * pair + 2, :].rearrange("p g (r t) -> p g r t", t=4),
-                in0=bank[:].rearrange("p g t r -> p g r t"),
-                in1=tiles["c", "spread"][:].unsqueeze(1).unsqueeze(3).to_broadcast([P, 2, P, 4]),
-                op=ALU.mult,
-            )
+        def copy_query(pair, bank):
+            out = q_grouped[:, 2 * pair : 2 * pair + 2, :].bitcast(F32).rearrange("p g (r u) -> p g r u", u=2)
+            src = bank[:].rearrange("p g u r -> p g r u")
+            if pair % 2 == 0:
+                nc.vector.tensor_copy(out=out, in_=src)
+            else:
+                nc.scalar.copy(out=out, in_=src)
+
+        def transpose_context(pair, tag):
+            bank = psum.tile([P, 2, 4, P], BF16, name="c_ps%d" % pair, tag=tag)
+            for gi in range(2):
+                base = 512 * (2 * (pair % 2) + gi)
+                for t in range(4):
+                    nc.tensor.transpose(
+                        bank[:, gi, t, :],
+                        y_sb["c", pair // 2][:, base + 128 * t : base + 128 * (t + 1)],
+                        ident_b[:],
+                    )
+            return bank
+
+        def copy_context(pair, bank):
+            out = c_grouped[:, 2 * pair : 2 * pair + 2, :].rearrange("p g (r t) -> p g r t", t=4)
+            src = bank[:].rearrange("p g t r -> p g r t")
+            if pair % 2 == 0:
+                nc.vector.tensor_copy(out=out, in_=src)
+            else:
+                nc.scalar.copy(out=out, in_=src)
 
         def quantise_half(grouped, codes, plane, h):
             sel = slice(4 * h, 4 * h + 4)
@@ -213,26 +218,29 @@ def tile_hyphawkes_w_kernel(tc, query, context, W_words, W_scales, c, out):
                 in_=grouped[:, sel, :].rearrange("p g x -> p (g x)"),
             )
 
-        factor_a("q", 0)
-        square("c", 0, 2)
-        square("c", 1, 3)
-        factor_b("q")
-        spread_q = factor_c("q", "bank4")
-        factor_d("q", spread_q)
-        for g in range(5):
-            scale_query(g)
+        square("q")
+        factor("q")
+        scale("q", 0)
+        scale("q", 1)
+        q_ps = [transpose_query(pair) for pair in range(4)]
+        copy_query(0, q_ps[0])
+        copy_query(1, q_ps[1])
+        copy_query(2, q_ps[2])
         quantise_half(q_grouped, q_codes, q_plane, 0)
-        for g in range(5, GROUPS):
-            scale_query(g)
-        factor_a("c", 2)
+        copy_query(3, q_ps[3])
         quantise_half(q_grouped, q_codes, q_plane, 1)
-        factor_b("c")
+        square("c")
+        factor("c")
+        scale("c", 0)
+        scale("c", 1)
 
         h_ps = {}
 
         def first_matmul(i, ranges):
             g, n0, n1 = PIECES[i]
             for j in ranges:
+                if 512 * j + 512 <= n0 or 512 * j >= n1:
+                    continue
                 if g == 0:
                     h_ps[j] = psum.tile([P, 4, P], F32, name="h_ps%d" % j, tag="bank%d" % BANK_OF_RANGE[j])
                 for t in range(4):
@@ -282,45 +290,43 @@ def tile_hyphawkes_w_kernel(tc, query, context, W_words, W_scales, c, out):
                 stop=(j == GROUPS - 1),
             )
 
-        first_matmul(0, range(7))
-        spread_c = factor_c("c", "bank7")
-        factor_d("c", spread_c)
+        for i in range(4):
+            first_matmul(i, range(7))
         for pair in range(4):
-            if pair > 0:
-                first_matmul(pair, range(7))
-            scale_context(pair, transpose_context(pair, "bank7"))
+            copy_context(pair, transpose_context(pair, "bank7"))
+            first_matmul(4 + pair, range(7))
         quantise_half(c_grouped, c_codes, c_plane, 0)
         quantise_half(c_grouped, c_codes, c_plane, 1)
-        for i in range(4):
-            first_matmul(i, [7])
-        first_matmul(4, range(8))
-        first_matmul(5, range(8))
-        first_matmul(6, range(4))
-        first_matmul(7, range(4))
+        for g in range(4):
+            first_matmul(2 * g + 1, [7])
+        for i in range(8, 12):
+            first_matmul(i, range(8))
+        first_matmul(12, range(4))
+        first_matmul(13, range(4))
         round_h(0)
         round_h(1)
         round_h(2)
         round_h(3)
-        first_matmul(8, [4, 5])
+        first_matmul(14, [4, 5])
         quantise_h(0)
         quantise_h(1)
         second_matmul(0)
         second_matmul(1)
-        first_matmul(9, [4, 5])
+        first_matmul(15, [4, 5])
         quantise_h(2)
         quantise_h(3)
         second_matmul(2)
         second_matmul(3)
         round_h(4)
         round_h(5)
-        first_matmul(10, [6, 7])
-        first_matmul(11, [6])
+        first_matmul(16, [6, 7])
+        first_matmul(17, [6])
         quantise_h(4)
         quantise_h(5)
         second_matmul(4)
         second_matmul(5)
-        first_matmul(12, [7])
-        first_matmul(13, [7])
+        first_matmul(18, [7])
+        first_matmul(19, [7])
         round_h(6)
         round_h(7)
         quantise_h(6)

@@ -22,10 +22,15 @@ FLOPS = 2 * P * D * D + 2 * P * P * D
 
 BANK_OF_RANGE = [4, 5, 6, 0, 1, 2, 3, 7]
 
-PIECES = (
-    [(g, n0, n0 + 2048) for g in range(6) for n0 in (0, 2048)]
-    + [(6, 0, 2048), (7, 0, 2048), (6, 2048, 3072), (7, 2048, 3072), (6, 3072, D), (7, 3072, 3584), (7, 3584, 3968), (7, 3968, D)]
-)
+PIECES = [(g, g + 1, 0, D) for g in range(6)] + [
+    (6, 7, 0, 2048),
+    (7, 8, 0, 2048),
+    (6, 7, 2048, D),
+    (7, 8, 2048, 3072),
+    (7, 8, 3072, 3584),
+    (7, 8, 3584, 3968),
+    (7, 8, 3968, D),
+]
 
 
 def tile_hyphawkes_w_kernel(tc, query, context, W_words, W_scales, c, out):
@@ -45,42 +50,30 @@ def tile_hyphawkes_w_kernel(tc, query, context, W_words, W_scales, c, out):
         nc.vector.memset(warm_in[:], 0.0)
         nc.scalar.activation(out=warm_out[:], in_=warm_in[:], func=ACT.Exp)
 
-        w_planes = keep.tile([P, 2, D], U8, name="w_planes", align_bytes=64)
-        for a in range(2):
-            nc.vector.memset(w_planes[:, a, :].bitcast(I32), 0)
+        w_planes = [keep.tile([P, D], U8, name="w_planes%d" % a, align_bytes=64) for a in range(2)]
+        nc.vector.memset(w_planes[1][:].bitcast(I32), 0)
+
+        for quad in (0, 2, 1, 3):
+            nc.sync.dma_start(
+                out=w_planes[0][32 * quad : 32 * quad + 32, :].bitcast(I32),
+                in_=W_scales[:, 4 * quad : 4 * quad + 4, :].bitcast(I32),
+            )
 
         x_sb = {}
+        for name, src in (("q", query), ("c", context)):
+            x_sb[name] = keep.tile([P, D], BF16, name="x_%s" % name, align_bytes=64)
+            nc.sync.dma_start(out=x_sb[name][:], in_=src[:, :])
+
+        nc.sync.dma_start(out=w_planes[1][0 : P - 16, :].bitcast(I32), in_=w_planes[0][16:P, :].bitcast(I32))
+
         w_sb = []
-
-        def load_x(name, src):
-            for h in range(2):
-                x_sb[name, h] = keep.tile([P, 2048], BF16, name="x_%s%d" % (name, h), align_bytes=64)
-                nc.sync.dma_start(out=x_sb[name, h][:], in_=src[:, 2048 * h : 2048 * (h + 1)])
-
-        def load_planes(a):
-            for quad in (0, 2, 1, 3):
-                nc.sync.dma_start(
-                    out=w_planes[32 * quad : 32 * quad + 16, a, :].bitcast(I32),
-                    in_=W_scales[4 * a : 4 * a + 4, 4 * quad : 4 * quad + 4, :].bitcast(I32),
-                )
-
-        def load_words(i):
-            g, n0, n1 = PIECES[i]
-            w_piece = keep.tile([P, n1 - n0], I32, name="w_%d" % i, align_bytes=64)
+        for i, (g0, g1, n0, n1) in enumerate(PIECES):
+            w_piece = keep.tile([P, g1 - g0, n1 - n0], I32, name="w_%d" % i, align_bytes=64)
             nc.sync.dma_start(
                 out=w_piece[:],
-                in_=W_words[g].rearrange("p n t -> p (n t)").bitcast(I32)[:, n0:n1],
+                in_=W_words[g0:g1].rearrange("g p n t -> p g (n t)").bitcast(I32)[:, :, n0:n1],
             )
             w_sb.append(w_piece)
-
-        load_x("q", query)
-        load_planes(0)
-        load_words(0)
-        load_words(1)
-        load_x("c", context)
-        load_planes(1)
-        for i in range(2, len(PIECES)):
-            load_words(i)
 
         ident_f = keep.tile([P, P], F32, name="ident_f")
         make_identity(nc, ident_f[:])
@@ -117,12 +110,12 @@ def tile_hyphawkes_w_kernel(tc, query, context, W_words, W_scales, c, out):
                 tiles[name, part] = small("%s_%s" % (part, name))
 
         def square(name):
-            nc.scalar.activation(out=junk[:], in_=x_sb[name, 0][:], func=ACT.Square, accum_out=sumsq[name, 0][:])
+            nc.scalar.activation(out=junk[:], in_=x_sb[name][:, 0:2048], func=ACT.Square, accum_out=sumsq[name, 0][:])
             nc.vector.scalar_tensor_tensor(
                 out=junk_v[:],
-                in0=x_sb[name, 1][:],
+                in0=x_sb[name][:, 2048:D],
                 scalar=1.0,
-                in1=x_sb[name, 1][:],
+                in1=x_sb[name][:, 2048:D],
                 op0=ALU.mult,
                 op1=ALU.mult,
                 accum_out=sumsq[name, 1][:],
@@ -163,7 +156,11 @@ def tile_hyphawkes_w_kernel(tc, query, context, W_words, W_scales, c, out):
         def scale(name, h):
             y_sb[name, h] = keep.tile([P, 2048], BF16, name="y_%s%d" % (name, h), align_bytes=64)
             nc.vector.tensor_scalar(
-                out=y_sb[name, h][:], in0=x_sb[name, h][:], scalar1=tiles[name, "s"][:, 0:1], scalar2=None, op0=ALU.mult
+                out=y_sb[name, h][:],
+                in0=x_sb[name][:, 2048 * h : 2048 * (h + 1)],
+                scalar1=tiles[name, "s"][:, 0:1],
+                scalar2=None,
+                op0=ALU.mult,
             )
 
         q_grouped = keep.tile([P, GROUPS, 512], BF16, name="q_grouped", align_bytes=64)
@@ -236,21 +233,20 @@ def tile_hyphawkes_w_kernel(tc, query, context, W_words, W_scales, c, out):
 
         h_ps = {}
 
-        def first_matmul(i, ranges):
-            g, n0, n1 = PIECES[i]
+        def first_matmul(g, ranges):
             for j in ranges:
-                if 512 * j + 512 <= n0 or 512 * j >= n1:
-                    continue
+                i = [g0 <= g < g1 and n0 <= 512 * j < n1 for g0, g1, n0, n1 in PIECES].index(True)
                 if g == 0:
                     h_ps[j] = psum.tile([P, 4, P], F32, name="h_ps%d" % j, tag="bank%d" % BANK_OF_RANGE[j])
                 for t in range(4):
                     col = 512 * j + 128 * t
-                    if col < n0 or col >= n1:
-                        continue
+                    if col >= PIECES[i][3]:
+                        i += 1
+                    g0, g1, n0, n1 = PIECES[i]
                     nc.tensor.matmul_mx(
                         out=h_ps[j][:, t, :],
-                        lhsT=w_sb[i][:, col - n0 : col - n0 + P].bitcast(FP8X4),
-                        lhsT_scale=w_planes[4 * (g % 4) : P, g // 4, col : col + P],
+                        lhsT=w_sb[i][:, g - g0, col - n0 : col - n0 + P].bitcast(FP8X4),
+                        lhsT_scale=w_planes[g // 4][4 * (g % 4) : P, col : col + P],
                         rhs=q_codes[:, g, :].bitcast(FP8X4),
                         rhs_scale=q_plane[:, g, :],
                         start=(g == 0 and t == 0),
@@ -290,49 +286,39 @@ def tile_hyphawkes_w_kernel(tc, query, context, W_words, W_scales, c, out):
                 stop=(j == GROUPS - 1),
             )
 
-        for i in range(4):
-            first_matmul(i, range(7))
+        first_matmul(0, range(7))
+        first_matmul(1, range(7))
         for pair in range(4):
             copy_context(pair, transpose_context(pair, "bank7"))
-            first_matmul(4 + pair, range(7))
+            first_matmul(2 + pair // 2, (range(4), range(4, 7))[pair % 2])
         quantise_half(c_grouped, c_codes, c_plane, 0)
         quantise_half(c_grouped, c_codes, c_plane, 1)
         for g in range(4):
-            first_matmul(2 * g + 1, [7])
-        for i in range(8, 12):
-            first_matmul(i, range(8))
-        first_matmul(12, range(4))
-        first_matmul(13, range(4))
-        round_h(0)
-        round_h(1)
-        round_h(2)
-        round_h(3)
-        first_matmul(14, [4, 5])
-        quantise_h(0)
-        quantise_h(1)
-        second_matmul(0)
-        second_matmul(1)
-        first_matmul(15, [4, 5])
-        quantise_h(2)
-        quantise_h(3)
-        second_matmul(2)
-        second_matmul(3)
+            first_matmul(g, [7])
+        first_matmul(4, range(8))
+        first_matmul(5, range(8))
+        first_matmul(6, range(4))
+        first_matmul(7, range(4))
+        for j in range(4):
+            round_h(j)
+        first_matmul(6, range(4, 8))
+        for j in range(4):
+            quantise_h(j)
+        for j in range(4):
+            second_matmul(j)
+        first_matmul(7, [4, 5])
         round_h(4)
         round_h(5)
-        first_matmul(16, [6, 7])
-        first_matmul(17, [6])
+        first_matmul(7, [6])
+        round_h(6)
         quantise_h(4)
         quantise_h(5)
-        second_matmul(4)
-        second_matmul(5)
-        first_matmul(18, [7])
-        first_matmul(19, [7])
-        round_h(6)
+        first_matmul(7, [7])
         round_h(7)
         quantise_h(6)
         quantise_h(7)
-        second_matmul(6)
-        second_matmul(7)
+        for j in range(4, 8):
+            second_matmul(j)
 
         neg = keep.tile([P, P], F32, name="neg")
         e = keep.tile([P, P], F32, name="e")

from contextlib import ExitStack

import concourse.mybir as mybir
from concourse.masks import make_identity

F32 = mybir.dt.float32
BF16 = mybir.dt.bfloat16
I32 = mybir.dt.int32
U32 = mybir.dt.uint32
U8 = mybir.dt.uint8
FP8X4 = mybir.dt.float8_e4m3fn_x4
ALU = mybir.AluOpType
ACT = mybir.ActivationFunctionType

P = 128
D = 4096
GROUPS = D // 512
MIN_NORM = 1e-5
BALL = 1.0 - 4e-3

FLOPS = 2 * P * D * D + 2 * P * P * D

BANK_OF_RANGE = [4, 5, 6, 0, 1, 2, 3, 7]

PIECES = [(g, g + 1, 0, D) for g in range(6)] + [
    (6, 7, 0, 2048),
    (7, 8, 0, 2048),
    (6, 7, 2048, D),
    (7, 8, 2048, 3072),
    (7, 8, 3072, 3584),
    (7, 8, 3584, 3968),
    (7, 8, 3968, D),
]


def tile_hyphawkes_w_kernel(tc, query, context, W_words, W_scales, c, out):
    nc = tc.nc
    with ExitStack() as stack:
        keep = stack.enter_context(tc.tile_pool(name="keep", bufs=1))
        psum = stack.enter_context(tc.psum_pool(name="psum", bufs=1))
        stack.enter_context(tc.manual_schedule())

        def small(name):
            return keep.tile([P, 1], F32, name=name)

        c_bf = keep.tile([P, 1], BF16, name="c_bf")
        nc.scalar.dma_start(out=c_bf[:], in_=c.partition_broadcast(P))
        warm_in = small("warm_in")
        warm_out = small("warm_out")
        nc.vector.memset(warm_in[:], 0.0)
        nc.scalar.activation(out=warm_out[:], in_=warm_in[:], func=ACT.Exp)

        w_planes = [keep.tile([P, D], U8, name="w_planes%d" % a, align_bytes=64) for a in range(2)]
        nc.vector.memset(w_planes[1][:].bitcast(I32), 0)

        for quad in (0, 2, 1, 3):
            nc.sync.dma_start(
                out=w_planes[0][32 * quad : 32 * quad + 32, :].bitcast(I32),
                in_=W_scales[:, 4 * quad : 4 * quad + 4, :].bitcast(I32),
            )

        x_sb = {}
        for name, src in (("q", query), ("c", context)):
            x_sb[name] = keep.tile([P, D], BF16, name="x_%s" % name, align_bytes=64)
            nc.sync.dma_start(out=x_sb[name][:], in_=src[:, :])

        nc.sync.dma_start(out=w_planes[1][0 : P - 16, :].bitcast(I32), in_=w_planes[0][16:P, :].bitcast(I32))

        w_sb = []
        for i, (g0, g1, n0, n1) in enumerate(PIECES):
            w_piece = keep.tile([P, g1 - g0, n1 - n0], I32, name="w_%d" % i, align_bytes=64)
            nc.sync.dma_start(
                out=w_piece[:],
                in_=W_words[g0:g1].rearrange("g p n t -> p g (n t)").bitcast(I32)[:, :, n0:n1],
            )
            w_sb.append(w_piece)

        ident_f = keep.tile([P, P], F32, name="ident_f")
        make_identity(nc, ident_f[:])
        ident_b = keep.tile([P, P], BF16, name="ident_b")
        make_identity(nc, ident_b[:])
        half = small("half")
        nc.gpsimd.memset(half[:], 0.5)
        neg_half = small("neg_half")
        nc.gpsimd.memset(neg_half[:], -0.5)

        c_f = small("c_f")
        root_c = small("root_c")
        inv_root_c = small("inv_root_c")
        radius = small("radius")
        cap = small("cap")
        gain = small("gain")
        nc.vector.tensor_copy(out=c_f[:], in_=c_bf[:])
        nc.gpsimd.tensor_tensor(out=root_c[:], in0=c_f[:], in1=half[:], op=ALU.pow)
        nc.vector.reciprocal(out=inv_root_c[:], in_=root_c[:])
        nc.vector.tensor_scalar(out=radius[:], in0=inv_root_c[:], scalar1=BALL, scalar2=None, op0=ALU.mult)
        nc.vector.tensor_scalar(
            out=cap[:], in0=radius[:], scalar1=1.0 / MIN_NORM, scalar2=1.0, op0=ALU.mult, op1=ALU.min
        )
        nc.vector.tensor_scalar(out=gain[:], in0=cap[:], scalar1=inv_root_c[:, 0:1], scalar2=None, op0=ALU.mult)

        junk = keep.tile([P, 2048], BF16, name="junk")
        junk_v = keep.tile([P, 2048], BF16, name="junk_v")
        sumsq = {}
        tiles = {}
        for name in ("q", "c"):
            sumsq[name, 0] = small("sumsq_%s0" % name)
            sumsq[name, 1] = small("sumsq_%s1" % name)
            for part in ("m", "r", "th", "rr", "t2", "s"):
                tiles[name, part] = small("%s_%s" % (part, name))

        def square(name):
            nc.scalar.activation(out=junk[:], in_=x_sb[name][:, 0:2048], func=ACT.Square, accum_out=sumsq[name, 0][:])
            nc.vector.scalar_tensor_tensor(
                out=junk_v[:],
                in0=x_sb[name][:, 2048:D],
                scalar=1.0,
                in1=x_sb[name][:, 2048:D],
                op0=ALU.mult,
                op1=ALU.mult,
                accum_out=sumsq[name, 1][:],
            )

        def factor(name):
            nc.vector.tensor_scalar(
                out=tiles[name, "m"][:],
                in0=sumsq[name, 0][:],
                scalar1=sumsq[name, 1][:, 0:1],
                scalar2=MIN_NORM * MIN_NORM,
                op0=ALU.add,
                op1=ALU.max,
            )
            nc.gpsimd.tensor_tensor(out=tiles[name, "r"][:], in0=tiles[name, "m"][:], in1=half[:], op=ALU.pow)
            nc.scalar.activation(
                out=tiles[name, "th"][:], in_=tiles[name, "r"][:], func=ACT.Tanh, scale=root_c[:, 0:1]
            )
            nc.vector.reciprocal(out=tiles[name, "rr"][:], in_=tiles[name, "r"][:])
            nc.vector.tensor_scalar(
                out=tiles[name, "t2"][:],
                in0=tiles[name, "th"][:],
                scalar1=gain[:, 0:1],
                scalar2=radius[:, 0:1],
                op0=ALU.mult,
                op1=ALU.min,
            )
            nc.vector.tensor_scalar(
                out=tiles[name, "s"][:],
                in0=tiles[name, "t2"][:],
                scalar1=tiles[name, "rr"][:, 0:1],
                scalar2=None,
                op0=ALU.mult,
            )

        y_sb = {}

        def scale(name, h):
            y_sb[name, h] = keep.tile([P, 2048], BF16, name="y_%s%d" % (name, h), align_bytes=64)
            nc.vector.tensor_scalar(
                out=y_sb[name, h][:],
                in0=x_sb[name][:, 2048 * h : 2048 * (h + 1)],
                scalar1=tiles[name, "s"][:, 0:1],
                scalar2=None,
                op0=ALU.mult,
            )

        q_grouped = keep.tile([P, GROUPS, 512], BF16, name="q_grouped", align_bytes=64)
        q_codes = keep.tile([P, GROUPS, P], U32, name="q_codes", align_bytes=64)
        q_plane = keep.tile([P, GROUPS, P], U8, name="q_plane", align_bytes=64)
        c_grouped = keep.tile([P, GROUPS, 512], BF16, name="c_grouped", align_bytes=64)
        c_codes = keep.tile([P, GROUPS, P], U32, name="c_codes", align_bytes=64)
        c_plane = keep.tile([P, GROUPS, P], U8, name="c_plane", align_bytes=64)

        def transpose_query(pair):
            bank = psum.tile([P, 2, 2, P], F32, name="q_ps%d" % pair, tag="bank%d" % pair)
            words = y_sb["q", pair // 2][:].bitcast(F32)
            for gi in range(2):
                base = 256 * (2 * (pair % 2) + gi)
                for u in range(2):
                    nc.tensor.transpose(bank[:, gi, u, :], words[:, base + u : base + 256 : 2], ident_f[:])
            return bank

        def copy_query(pair, bank):
            out = q_grouped[:, 2 * pair : 2 * pair + 2, :].bitcast(F32).rearrange("p g (r u) -> p g r u", u=2)
            src = bank[:].rearrange("p g u r -> p g r u")
            if pair % 2 == 0:
                nc.vector.tensor_copy(out=out, in_=src)
            else:
                nc.scalar.copy(out=out, in_=src)

        def transpose_context(pair, tag):
            bank = psum.tile([P, 2, 4, P], BF16, name="c_ps%d" % pair, tag=tag)
            for gi in range(2):
                base = 512 * (2 * (pair % 2) + gi)
                for t in range(4):
                    nc.tensor.transpose(
                        bank[:, gi, t, :],
                        y_sb["c", pair // 2][:, base + 128 * t : base + 128 * (t + 1)],
                        ident_b[:],
                    )
            return bank

        def copy_context(pair, bank):
            out = c_grouped[:, 2 * pair : 2 * pair + 2, :].rearrange("p g (r t) -> p g r t", t=4)
            src = bank[:].rearrange("p g t r -> p g r t")
            if pair % 2 == 0:
                nc.vector.tensor_copy(out=out, in_=src)
            else:
                nc.scalar.copy(out=out, in_=src)

        def quantise_half(grouped, codes, plane, h):
            sel = slice(4 * h, 4 * h + 4)
            nc.vector.quantize_mx(
                out=codes[:, sel, :].rearrange("p g r -> p (g r)").bitcast(FP8X4),
                scales=plane[:, sel, :].rearrange("p g r -> p (g r)"),
                in_=grouped[:, sel, :].rearrange("p g x -> p (g x)"),
            )

        square("q")
        factor("q")
        scale("q", 0)
        scale("q", 1)
        q_ps = [transpose_query(pair) for pair in range(4)]
        copy_query(0, q_ps[0])
        copy_query(1, q_ps[1])
        copy_query(2, q_ps[2])
        quantise_half(q_grouped, q_codes, q_plane, 0)
        copy_query(3, q_ps[3])
        quantise_half(q_grouped, q_codes, q_plane, 1)
        square("c")
        factor("c")
        scale("c", 0)
        scale("c", 1)

        h_ps = {}

        def first_matmul(g, ranges):
            for j in ranges:
                i = [g0 <= g < g1 and n0 <= 512 * j < n1 for g0, g1, n0, n1 in PIECES].index(True)
                if g == 0:
                    h_ps[j] = psum.tile([P, 4, P], F32, name="h_ps%d" % j, tag="bank%d" % BANK_OF_RANGE[j])
                for t in range(4):
                    col = 512 * j + 128 * t
                    if col >= PIECES[i][3]:
                        i += 1
                    g0, g1, n0, n1 = PIECES[i]
                    nc.tensor.matmul_mx(
                        out=h_ps[j][:, t, :],
                        lhsT=w_sb[i][:, g - g0, col - n0 : col - n0 + P].bitcast(FP8X4),
                        lhsT_scale=w_planes[g // 4][4 * (g % 4) : P, col : col + P],
                        rhs=q_codes[:, g, :].bitcast(FP8X4),
                        rhs_scale=q_plane[:, g, :],
                        start=(g == 0 and t == 0),
                        stop=(g == GROUPS - 1 and t == 3),
                    )

        h_grouped = [keep.tile([P, P, 4], BF16, name="h_grouped%d" % j, align_bytes=64) for j in range(GROUPS)]
        h_codes = [keep.tile([P, P], U32, name="h_codes%d" % j, align_bytes=64) for j in range(GROUPS)]
        h_plane = [keep.tile([P, P], U8, name="h_plane%d" % j, align_bytes=64) for j in range(GROUPS)]

        def round_h(j):
            src = h_ps[j][:].rearrange("p t r -> p r t")
            if j % 2 == 0:
                nc.vector.tensor_copy(out=h_grouped[j][:], in_=src)
            else:
                nc.scalar.copy(out=h_grouped[j][:], in_=src)

        def quantise_h(j):
            nc.vector.quantize_mx(
                out=h_codes[j][:].bitcast(FP8X4),
                scales=h_plane[j][:],
                in_=h_grouped[j][:].rearrange("p r t -> p (r t)"),
            )

        scores = []

        def second_matmul(j):
            if j == 0:
                scores.append(psum.tile([P, P], F32, name="scores", tag="bank%d" % BANK_OF_RANGE[0]))
            nc.tensor.matmul_mx(
                out=scores[0][:],
                lhsT=h_codes[j][:].bitcast(FP8X4),
                lhsT_scale=h_plane[j][:],
                rhs=c_codes[:, j, :].bitcast(FP8X4),
                rhs_scale=c_plane[:, j, :],
                start=(j == 0),
                stop=(j == GROUPS - 1),
            )

        first_matmul(0, range(7))
        first_matmul(1, range(7))
        for pair in range(4):
            copy_context(pair, transpose_context(pair, "bank7"))
            first_matmul(2 + pair // 2, (range(4), range(4, 7))[pair % 2])
        quantise_half(c_grouped, c_codes, c_plane, 0)
        quantise_half(c_grouped, c_codes, c_plane, 1)
        for g in range(4):
            first_matmul(g, [7])
        first_matmul(4, range(8))
        first_matmul(5, range(8))
        first_matmul(6, range(4))
        first_matmul(7, range(4))
        for j in range(4):
            round_h(j)
        first_matmul(6, range(4, 8))
        for j in range(4):
            quantise_h(j)
        for j in range(4):
            second_matmul(j)
        first_matmul(7, [4, 5])
        round_h(4)
        round_h(5)
        first_matmul(7, [6])
        round_h(6)
        quantise_h(4)
        quantise_h(5)
        first_matmul(7, [7])
        round_h(7)
        quantise_h(6)
        quantise_h(7)
        for j in range(4, 8):
            second_matmul(j)

        neg = keep.tile([P, P], F32, name="neg")
        e = keep.tile([P, P], F32, name="e")
        e2 = keep.tile([P, P], F32, name="e2")
        res = keep.tile([P, P], F32, name="res")
        shift = small("shift")
        total = small("total")
        total2 = small("total2")
        arg2 = small("arg2")
        shift1 = small("shift1")
        e_gain = keep.tile([P, P], F32, name="e_gain")
        e_cap = keep.tile([P, P], F32, name="e_cap")
        inv_total = small("inv_total")
        arg_scale = small("arg_scale")
        th = small("th")
        inv_root2 = small("inv_root2")
        nc.vector.tensor_scalar(
            out=neg[:], in0=scores[0][:], scalar1=-2.0 / D, scalar2=None, op0=ALU.mult, op1=ALU.min, accum_out=shift[:]
        )
        nc.scalar.activation(out=e2[:], in_=neg[:], func=ACT.Exp, scale=-1.0, bias=shift[:, 0:1], accum_out=total2[:])
        nc.vector.tensor_scalar(out=shift1[:], in0=shift[:], scalar1=0.5, scalar2=None, op0=ALU.mult)
        nc.scalar.activation(out=e[:], in_=neg[:], func=ACT.Exp, scale=-0.5, bias=shift1[:, 0:1], accum_out=total[:])
        nc.gpsimd.tensor_tensor(out=inv_root2[:], in0=total2[:], in1=neg_half[:], op=ALU.pow)
        nc.vector.tensor_scalar(
            out=arg_scale[:], in0=total2[:], scalar1=root_c[:, 0:1], scalar2=None, op0=ALU.mult
        )
        nc.vector.reciprocal(out=inv_total[:], in_=total[:])
        nc.vector.tensor_scalar(
            out=arg2[:], in0=inv_total[:], scalar1=arg_scale[:, 0:1], scalar2=None, op0=ALU.mult
        )
        nc.scalar.activation(out=th[:], in_=inv_root2[:], func=ACT.Tanh, scale=arg2[:, 0:1])
        nc.vector.tensor_scalar(
            out=e_gain[:], in0=e[:], scalar1=gain[:, 0:1], scalar2=inv_root2[:, 0:1], op0=ALU.mult, op1=ALU.mult
        )
        nc.vector.tensor_scalar(
            out=e_cap[:], in0=e[:], scalar1=radius[:, 0:1], scalar2=inv_root2[:, 0:1], op0=ALU.mult, op1=ALU.mult
        )
        nc.vector.scalar_tensor_tensor(
            out=res[:], in0=e_gain[:], scalar=th[:, 0:1], in1=e_cap[:], op0=ALU.mult, op1=ALU.min
        )
        nc.sync.dma_start(out=out[:, :], in_=res[:])
